import numpy as np
import ml_dtypes


def mxq(x, axis, fmt="e4m3"):
    dtype, down = {"e4m3": (ml_dtypes.float8_e4m3fn, 7), "e5m2": (ml_dtypes.float8_e5m2, 14)}[fmt]
    v = np.moveaxis(np.asarray(x, np.float32).astype(ml_dtypes.bfloat16).astype(np.float64), axis, -1)
    blocks = v.reshape(v.shape[:-1] + (-1, 32))
    amax = np.abs(blocks).max(-1, keepdims=True)
    byte = np.maximum(np.where(amax > 0, np.frexp(amax)[1] - 1 + 127, 0) - down, 1)
    scale = np.exp2(byte - 127.0)
    codes = (blocks / scale).astype(np.float32).astype(dtype).astype(np.float64)
    return np.moveaxis((codes * scale).reshape(v.shape), -1, axis)


WIDE = False


def mx_kscale(k):
    if not WIDE:
        return np.ones(k)
    levels = np.array([10, -10, 5, -5, 0])
    a = np.random.permutation(np.resize(levels, k // 512 * 4)).reshape(k // 512, 4)
    idx = np.arange(k)
    return np.exp2(a[idx // 512, idx % 128 // 32])


BF16 = ml_dtypes.bfloat16


def bf(x):
    return np.asarray(x, np.float32).astype(BF16)


def f64(x):
    return np.asarray(x).astype(np.float64)


E2M1 = np.array([0.0, 0.5, 1.0, 1.5, 2.0, 3.0, 4.0, 6.0, -0.0, -0.5, -1.0, -1.5, -2.0, -3.0, -4.0, -6.0])


def pack_weight(w, fmt):
    k, n = w.shape
    w = f64(bf(w)).reshape(k // 32, 32, n)
    amax = np.abs(w).max(1)
    if fmt == "e4m3":
        byte = np.frexp(amax)[1] - 1 + 127 - 7
    else:
        mant, ex = np.frexp(amax / 6.0)
        byte = np.where(mant > 0.5, ex, ex - 1) + 127
    byte = np.clip(np.where(amax > 0, byte, 1), 1, 254)
    scaled = (w * np.exp2(127.0 - byte)[:, None, :]).reshape(k, n).astype(np.float32)
    by_word = np.ascontiguousarray(scaled.reshape(k // 512, 128, 4, n).transpose(0, 1, 3, 2))
    if fmt == "e4m3":
        words = by_word.astype(ml_dtypes.float8_e4m3fn).view(np.uint8)
    else:
        c = by_word.astype(ml_dtypes.float4_e2m1fn).view(np.uint8) & 0xF
        words = c[..., 0::2] | (c[..., 1::2] << 4)
    return np.ascontiguousarray(words), np.ascontiguousarray(byte.astype(np.uint8).reshape(k // 512, 16, n))


def unpack_weight(words, scales, fmt):
    g, p, n, _ = words.shape
    if fmt == "e4m3":
        vals = np.ascontiguousarray(words).view(ml_dtypes.float8_e4m3fn).astype(np.float64)
    else:
        nib = np.empty((g, p, n, 4), np.uint8)
        nib[..., 0::2] = words & 0xF
        nib[..., 1::2] = words >> 4
        vals = E2M1[nib]
    vals = vals * np.repeat(np.exp2(scales.astype(np.float64) - 127.0), 8, axis=1)[..., None]
    return vals.transpose(0, 1, 3, 2).reshape(g * 512, n)

def pack4(w):
    words, scales = pack_weight(w, "e2m1")
    return words.reshape(words.shape[0], 128, -1), scales


def unpack4(words, scales):
    return unpack_weight(words.reshape(words.shape[0], 128, -1, 2), scales, "e2m1")


BATCH, IN_F, OUT_F, RANK, N_ADAPTERS = 8192, 512, 512, 128, 8
SEG = BATCH // N_ADAPTERS
LORA_GAIN = 2.0


def setup_inputs():
    s = mx_kscale(IN_F)
    x = bf(np.random.standard_normal((BATCH, IN_F)) * s)
    h_lora = bf(np.random.standard_normal((N_ADAPTERS, SEG, RANK)))
    lora_B = bf(np.random.standard_normal((N_ADAPTERS, RANK, OUT_F)) * 0.5 / np.sqrt(RANK))
    words, scales = pack4(np.random.standard_normal((IN_F, OUT_F)) / np.sqrt(IN_F) / s[:, None])
    return {"x": x,
            "h_lora": h_lora,
            "lora_B": lora_B,
            "M_words": words,
            "M_scales": scales}


def reference(x, h_lora, lora_B, M_words, M_scales):
    y = (f64(h_lora) @ f64(lora_B)) * LORA_GAIN
    y = y.reshape(BATCH, OUT_F)
    return y + (mxq(f64(x), 1, "e4m3") @ unpack4(M_words, M_scales))

@@ -1,0 +1,190 @@
+from contextlib import ExitStack
+
+import concourse.mybir as mybir
+from concourse.masks import make_identity
+
+BF16 = mybir.dt.bfloat16
+F32 = mybir.dt.float32
+I32 = mybir.dt.int32
+U8 = mybir.dt.uint8
+U32 = mybir.dt.uint32
+FP8X4 = mybir.dt.float8_e4m3fn_x4
+FP4X4 = mybir.dt.float4_e2m1fn_x4
+
+P = 128
+BATCH, IN_F, OUT_F, RANK, N_ADAPTERS = 8192, 512, 512, 128, 8
+LORA_GAIN = 2.0
+SEG_TILES = BATCH // N_ADAPTERS // P
+ROUND_TILES = 4
+SEG_ROUNDS = SEG_TILES // ROUND_TILES
+ROUNDS = N_ADAPTERS * SEG_ROUNDS
+K_WORDS = IN_F // 2
+STAGED_ROUNDS = 10
+
+FLOPS = 2 * BATCH * OUT_F * (IN_F + RANK)
+
+
+def tile_lorasequential_pa_t_kernel(tc, x, h_lora, lora_B, M_words, M_scales, out):
+    nc = tc.nc
+
+    x_rows = x.rearrange("(g p j) k -> g p j k", g=N_ADAPTERS, p=P)
+    h_rows = h_lora.rearrange("g (p j) k -> g p j k", p=P)
+    out_rows = out.rearrange("(g p j) n -> g p j n", g=N_ADAPTERS, p=P)
+
+    with ExitStack() as ctx:
+        ctx.enter_context(tc.manual_schedule())
+        consts = ctx.enter_context(tc.tile_pool(name="consts", bufs=1))
+        x_pool = ctx.enter_context(tc.tile_pool(name="x", bufs=ROUNDS))
+        seg_pool = ctx.enter_context(tc.tile_pool(name="seg", bufs=N_ADAPTERS))
+        work = ctx.enter_context(tc.tile_pool(name="work", bufs=2))
+        ht_pool = ctx.enter_context(tc.tile_pool(name="ht_sb", bufs=3))
+        staged = ctx.enter_context(tc.tile_pool(name="staged", bufs=STAGED_ROUNDS))
+        xt_banks = ctx.enter_context(tc.psum_pool(name="xt", bufs=2))
+        ht_banks = ctx.enter_context(tc.psum_pool(name="ht", bufs=1))
+        lora_banks = ctx.enter_context(tc.psum_pool(name="lora", bufs=2))
+        base_banks = ctx.enter_context(tc.psum_pool(name="base", bufs=3))
+
+        ident_f32 = consts.tile([P, P], F32)
+        make_identity(nc, ident_f32[:])
+        ident_bf16 = consts.tile([P, P], BF16)
+        make_identity(nc, ident_bf16[:])
+
+        m_words = consts.tile([P, 2 * OUT_F], U8, align_bytes=64)
+        m_scales = consts.tile([P, OUT_F], U8, align_bytes=64)
+        nc.vector.memset(m_scales[:].bitcast(I32), 0)
+
+        x_tiles = []
+        h_tiles = []
+        b_tiles = []
+
+        def load_x(r):
+            g, half = divmod(r, SEG_ROUNDS)
+            x_sb = x_pool.tile([P, ROUND_TILES, IN_F], BF16)
+            first = half * ROUND_TILES
+            nc.sync.dma_start(out=x_sb[:], in_=x_rows[g][:, first : first + ROUND_TILES, :])
+            x_tiles.append(x_sb)
+
+        def load_adapter(g):
+            h_sb = seg_pool.tile([P, SEG_TILES, RANK], BF16)
+            nc.sync.dma_start(out=h_sb[:], in_=h_rows[g])
+            h_tiles.append(h_sb)
+            b_sb = seg_pool.tile([P, OUT_F], BF16)
+            nc.sync.dma_start(out=b_sb[:], in_=lora_B[g])
+            b_tiles.append(b_sb)
+
+        def load_m():
+            nc.sync.dma_start(out=m_words[:].bitcast(I32), in_=M_words[0].bitcast(I32))
+            for quadrant in range(4):
+                nc.sync.dma_start(
+                    out=m_scales[32 * quadrant : 32 * quadrant + 4, :].bitcast(I32),
+                    in_=M_scales[0, 4 * quadrant : 4 * quadrant + 4, :].bitcast(I32),
+                )
+
+        for g in range(N_ADAPTERS):
+            load_x(SEG_ROUNDS * g)
+            load_adapter(g)
+            load_x(SEG_ROUNDS * g + 1)
+            if g == 0:
+                load_m()
+
+        hT_tiles = {}
+        grouped_tiles = {}
+        x_codes = {}
+        out_tiles = {}
+
+        def transpose_h(r):
+            g, half = divmod(r, SEG_ROUNDS)
+            ht_ps = ht_banks.tile([P, ROUND_TILES, P], BF16)
+            for i in range(ROUND_TILES):
+                nc.tensor.transpose(
+                    ht_ps[:, i, :], h_tiles[g][:, half * ROUND_TILES + i, :], ident_bf16[:]
+                )
+            hT_sb = ht_pool.tile([P, ROUND_TILES, P], BF16)
+            nc.vector.tensor_copy(out=hT_sb[:], in_=ht_ps[:])
+            hT_tiles[r] = hT_sb
+
+        def transpose_x(r):
+            x_words = x_tiles[r][:].bitcast(F32)
+            grouped = work.tile([P, ROUND_TILES * P * 4], BF16, align_bytes=64)
+            grouped_words = grouped[:].bitcast(F32).rearrange(
+                "p (i r u) -> p i r u", i=ROUND_TILES, u=2
+            )
+            for pair in range(ROUND_TILES // 2):
+                xt_ps = xt_banks.tile([P, 2, 2, P], F32)
+                for i in range(2):
+                    for u in range(2):
+                        nc.tensor.transpose(
+                            xt_ps[:, i, u, :], x_words[:, 2 * pair + i, u:K_WORDS:2], ident_f32[:]
+                        )
+                nc.scalar.copy(
+                    out=grouped_words[:, 2 * pair : 2 * pair + 2],
+                    in_=xt_ps[:].rearrange("p i u r -> p i r u"),
+                )
+            grouped_tiles[r] = grouped
+
+        def quantise_x(r):
+            codes = work.tile([P, ROUND_TILES * P], U32, align_bytes=64)
+            scales = work.tile([P, ROUND_TILES * P], U8, align_bytes=64)
+            nc.vector.quantize_mx(
+                out=codes[:].bitcast(FP8X4), scales=scales[:], in_=grouped_tiles[r][:]
+            )
+            x_codes[r] = (codes, scales)
+
+        def lora(r, i):
+            if i == 0:
+                out_sb = staged.tile([P, ROUND_TILES, OUT_F], F32)
+                out_tiles[r] = out_sb
+            lora_ps = lora_banks.tile([P, OUT_F], F32)
+            nc.tensor.matmul(
+                out=lora_ps[:],
+                lhsT=hT_tiles[r][:, i, :],
+                rhs=b_tiles[r // SEG_ROUNDS][:],
+                start=True,
+                stop=True,
+            )
+            nc.scalar.mul(out=out_tiles[r][:, i, :], in_=lora_ps[:], mul=LORA_GAIN)
+
+        def base(r, i):
+            codes, scales = x_codes[r]
+            rows = slice(i * P, (i + 1) * P)
+            base_ps = base_banks.tile([P, OUT_F], F32)
+            nc.tensor.matmul_mx(
+                out=base_ps[:],
+                lhsT=codes[:, rows].bitcast(FP8X4),
+                lhsT_scale=scales[:, rows],
+                rhs=m_words[:].bitcast(FP4X4),
+                rhs_scale=m_scales[:],
+                start=True,
+                stop=True,
+            )
+            out_sb = out_tiles[r]
+            nc.vector.tensor_add(out=out_sb[:, i, :], in0=base_ps[:], in1=out_sb[:, i, :])
+
+        def store(r, lo, hi):
+            g, half = divmod(r, SEG_ROUNDS)
+            first = half * ROUND_TILES
+            nc.sync.dma_start(
+                out=out_rows[g][:, first + lo : first + hi, :], in_=out_tiles[r][:, lo:hi, :]
+            )
+
+        transpose_x(0)
+        transpose_h(0)
+        transpose_h(1)
+        quantise_x(0)
+        for i in range(ROUND_TILES):
+            lora(0, i)
+        for r in range(ROUNDS):
+            if r + 1 < ROUNDS:
+                transpose_x(r + 1)
+            if r + 2 < ROUNDS:
+                transpose_h(r + 2)
+            for i in range(ROUND_TILES):
+                if r + 1 < ROUNDS:
+                    lora(r + 1, i)
+                base(r, i)
+                if i == ROUND_TILES // 2 - 1 and r + 1 < ROUNDS:
+                    quantise_x(r + 1)
+                if r == ROUNDS - 1:
+                    store(r, i, i + 1)
+            if r < ROUNDS - 1:
+                store(r, 0, ROUND_TILES)

@@ -39,10 +39,7 @@ def tile_lorasequential_pa_t_kernel(tc, x, h_lora, lora_B, M_words, M_scales, ou
         work = ctx.enter_context(tc.tile_pool(name="work", bufs=2))
         ht_pool = ctx.enter_context(tc.tile_pool(name="ht_sb", bufs=3))
         staged = ctx.enter_context(tc.tile_pool(name="staged", bufs=STAGED_ROUNDS))
-        xt_banks = ctx.enter_context(tc.psum_pool(name="xt", bufs=2))
-        ht_banks = ctx.enter_context(tc.psum_pool(name="ht", bufs=1))
-        lora_banks = ctx.enter_context(tc.psum_pool(name="lora", bufs=2))
-        base_banks = ctx.enter_context(tc.psum_pool(name="base", bufs=3))
+        banks = ctx.enter_context(tc.psum_pool(name="banks", bufs=8))
 
         ident_f32 = consts.tile([P, P], F32)
         make_identity(nc, ident_f32[:])
@@ -94,7 +91,7 @@ def tile_lorasequential_pa_t_kernel(tc, x, h_lora, lora_B, M_words, M_scales, ou
 
         def transpose_h(r):
             g, half = divmod(r, SEG_ROUNDS)
-            ht_ps = ht_banks.tile([P, ROUND_TILES, P], BF16)
+            ht_ps = banks.tile([P, ROUND_TILES, P], BF16, tag="bank")
             for i in range(ROUND_TILES):
                 nc.tensor.transpose(
                     ht_ps[:, i, :], h_tiles[g][:, half * ROUND_TILES + i, :], ident_bf16[:]
@@ -110,7 +107,7 @@ def tile_lorasequential_pa_t_kernel(tc, x, h_lora, lora_B, M_words, M_scales, ou
                 "p (i r u) -> p i r u", i=ROUND_TILES, u=2
             )
             for pair in range(ROUND_TILES // 2):
-                xt_ps = xt_banks.tile([P, 2, 2, P], F32)
+                xt_ps = banks.tile([P, 2, 2, P], F32, tag="bank")
                 for i in range(2):
                     for u in range(2):
                         nc.tensor.transpose(
@@ -134,7 +131,7 @@ def tile_lorasequential_pa_t_kernel(tc, x, h_lora, lora_B, M_words, M_scales, ou
             if i == 0:
                 out_sb = staged.tile([P, ROUND_TILES, OUT_F], F32)
                 out_tiles[r] = out_sb
-            lora_ps = lora_banks.tile([P, OUT_F], F32)
+            lora_ps = banks.tile([P, OUT_F], F32, tag="bank")
             nc.tensor.matmul(
                 out=lora_ps[:],
                 lhsT=hT_tiles[r][:, i, :],
@@ -147,7 +144,7 @@ def tile_lorasequential_pa_t_kernel(tc, x, h_lora, lora_B, M_words, M_scales, ou
         def base(r, i):
             codes, scales = x_codes[r]
             rows = slice(i * P, (i + 1) * P)
-            base_ps = base_banks.tile([P, OUT_F], F32)
+            base_ps = banks.tile([P, OUT_F], F32, tag="bank")
             nc.tensor.matmul_mx(
                 out=base_ps[:],
                 lhsT=codes[:, rows].bitcast(FP8X4),

@@ -19,6 +19,8 @@ ROUND_TILES = 4
 SEG_ROUNDS = SEG_TILES // ROUND_TILES
 ROUNDS = N_ADAPTERS * SEG_ROUNDS
 K_WORDS = IN_F // 2
+FINE_ROUNDS = 2
+WARM_MATMULS = 3
 STAGED_ROUNDS = 10
 
 FLOPS = 2 * BATCH * OUT_F * (IN_F + RANK)
@@ -34,7 +36,8 @@ def tile_lorasequential_pa_t_kernel(tc, x, h_lora, lora_B, M_words, M_scales, ou
     with ExitStack() as ctx:
         ctx.enter_context(tc.manual_schedule())
         consts = ctx.enter_context(tc.tile_pool(name="consts", bufs=1))
-        x_pool = ctx.enter_context(tc.tile_pool(name="x", bufs=ROUNDS))
+        x_pool = ctx.enter_context(tc.tile_pool(name="x", bufs=ROUNDS - 1))
+        first_pool = ctx.enter_context(tc.tile_pool(name="first", bufs=ROUND_TILES))
         seg_pool = ctx.enter_context(tc.tile_pool(name="seg", bufs=N_ADAPTERS))
         work = ctx.enter_context(tc.tile_pool(name="work", bufs=2))
         ht_pool = ctx.enter_context(tc.tile_pool(name="ht_sb", bufs=3))
@@ -46,6 +49,12 @@ def tile_lorasequential_pa_t_kernel(tc, x, h_lora, lora_B, M_words, M_scales, ou
         ident_bf16 = consts.tile([P, P], BF16)
         make_identity(nc, ident_bf16[:])
 
+        zeros = consts.tile([P, OUT_F], BF16)
+        nc.vector.memset(zeros[:], 0.0)
+        warm_ps = banks.tile([P, OUT_F], F32, tag="bank")
+        for w in range(WARM_MATMULS):
+            nc.tensor.matmul(out=warm_ps[:], lhsT=zeros[:, 0:P], rhs=zeros[:], start=True, stop=True)
+
         m_words = consts.tile([P, 2 * OUT_F], U8, align_bytes=64)
         m_scales = consts.tile([P, OUT_F], U8, align_bytes=64)
         nc.vector.memset(m_scales[:].bitcast(I32), 0)
@@ -56,10 +65,18 @@ def tile_lorasequential_pa_t_kernel(tc, x, h_lora, lora_B, M_words, M_scales, ou
 
         def load_x(r):
             g, half = divmod(r, SEG_ROUNDS)
-            x_sb = x_pool.tile([P, ROUND_TILES, IN_F], BF16)
             first = half * ROUND_TILES
-            nc.sync.dma_start(out=x_sb[:], in_=x_rows[g][:, first : first + ROUND_TILES, :])
-            x_tiles.append(x_sb)
+            if r == 0:
+                pieces = []
+                for i in range(ROUND_TILES):
+                    x_one = first_pool.tile([P, IN_F], BF16)
+                    nc.sync.dma_start(out=x_one[:], in_=x_rows[g][:, first + i, :])
+                    pieces.append(x_one[:].bitcast(F32))
+                x_tiles.append(pieces)
+            else:
+                x_sb = x_pool.tile([P, ROUND_TILES, IN_F], BF16)
+                nc.sync.dma_start(out=x_sb[:], in_=x_rows[g][:, first : first + ROUND_TILES, :])
+                x_tiles.append([x_sb[:, i, :].bitcast(F32) for i in range(ROUND_TILES)])
 
         def load_adapter(g):
             h_sb = seg_pool.tile([P, SEG_TILES, RANK], BF16)
@@ -101,7 +118,6 @@ def tile_lorasequential_pa_t_kernel(tc, x, h_lora, lora_B, M_words, M_scales, ou
             hT_tiles[r] = hT_sb
 
         def transpose_x(r):
-            x_words = x_tiles[r][:].bitcast(F32)
             grouped = work.tile([P, ROUND_TILES * P * 4], BF16, align_bytes=64)
             grouped_words = grouped[:].bitcast(F32).rearrange(
                 "p (i r u) -> p i r u", i=ROUND_TILES, u=2
@@ -111,7 +127,7 @@ def tile_lorasequential_pa_t_kernel(tc, x, h_lora, lora_B, M_words, M_scales, ou
                 for i in range(2):
                     for u in range(2):
                         nc.tensor.transpose(
-                            xt_ps[:, i, u, :], x_words[:, 2 * pair + i, u:K_WORDS:2], ident_f32[:]
+                            xt_ps[:, i, u, :], x_tiles[r][2 * pair + i][:, u:K_WORDS:2], ident_f32[:]
                         )
                 nc.scalar.copy(
                     out=grouped_words[:, 2 * pair : 2 * pair + 2],
@@ -181,7 +197,7 @@ def tile_lorasequential_pa_t_kernel(tc, x, h_lora, lora_B, M_words, M_scales, ou
                 base(r, i)
                 if i == ROUND_TILES // 2 - 1 and r + 1 < ROUNDS:
                     quantise_x(r + 1)
-                if r == ROUNDS - 1:
+                if r >= ROUNDS - FINE_ROUNDS:
                     store(r, i, i + 1)
-            if r < ROUNDS - 1:
+            if r < ROUNDS - FINE_ROUNDS:
                 store(r, 0, ROUND_TILES)

@@ -19,9 +19,8 @@ ROUND_TILES = 4
 SEG_ROUNDS = SEG_TILES // ROUND_TILES
 ROUNDS = N_ADAPTERS * SEG_ROUNDS
 K_WORDS = IN_F // 2
-FINE_ROUNDS = 2
 WARM_MATMULS = 3
-STAGED_ROUNDS = 10
+STAGED_SEGMENTS = 5
 
 FLOPS = 2 * BATCH * OUT_F * (IN_F + RANK)
 
@@ -36,12 +35,12 @@ def tile_lorasequential_pa_t_kernel(tc, x, h_lora, lora_B, M_words, M_scales, ou
     with ExitStack() as ctx:
         ctx.enter_context(tc.manual_schedule())
         consts = ctx.enter_context(tc.tile_pool(name="consts", bufs=1))
-        x_pool = ctx.enter_context(tc.tile_pool(name="x", bufs=ROUNDS - 1))
-        first_pool = ctx.enter_context(tc.tile_pool(name="first", bufs=ROUND_TILES))
+        x_pool = ctx.enter_context(tc.tile_pool(name="x", bufs=N_ADAPTERS - 1))
+        first_pool = ctx.enter_context(tc.tile_pool(name="first", bufs=1))
         seg_pool = ctx.enter_context(tc.tile_pool(name="seg", bufs=N_ADAPTERS))
         work = ctx.enter_context(tc.tile_pool(name="work", bufs=2))
         ht_pool = ctx.enter_context(tc.tile_pool(name="ht_sb", bufs=3))
-        staged = ctx.enter_context(tc.tile_pool(name="staged", bufs=STAGED_ROUNDS))
+        staged = ctx.enter_context(tc.tile_pool(name="staged", bufs=STAGED_SEGMENTS))
         banks = ctx.enter_context(tc.psum_pool(name="banks", bufs=8))
 
         ident_f32 = consts.tile([P, P], F32)
@@ -63,25 +62,21 @@ def tile_lorasequential_pa_t_kernel(tc, x, h_lora, lora_B, M_words, M_scales, ou
         h_tiles = []
         b_tiles = []
 
-        def load_x(r):
-            g, half = divmod(r, SEG_ROUNDS)
-            first = half * ROUND_TILES
-            if r == 0:
-                pieces = []
-                for i in range(ROUND_TILES):
-                    x_one = first_pool.tile([P, IN_F], BF16)
-                    nc.sync.dma_start(out=x_one[:], in_=x_rows[g][:, first + i, :])
-                    pieces.append(x_one[:].bitcast(F32))
-                x_tiles.append(pieces)
-            else:
-                x_sb = x_pool.tile([P, ROUND_TILES, IN_F], BF16)
-                nc.sync.dma_start(out=x_sb[:], in_=x_rows[g][:, first : first + ROUND_TILES, :])
-                x_tiles.append([x_sb[:, i, :].bitcast(F32) for i in range(ROUND_TILES)])
+        def load_x(g, cuts):
+            for lo, hi in zip(cuts[:-1], cuts[1:]):
+                if g == 0:
+                    x_sb = first_pool.tile([P, hi - lo, IN_F], BF16, name="x_first_%d" % lo)
+                else:
+                    x_sb = x_pool.tile([P, hi - lo, IN_F], BF16)
+                nc.sync.dma_start(out=x_sb[:], in_=x_rows[g][:, lo:hi, :])
+                x_tiles.extend([x_sb[:, j, :].bitcast(F32) for j in range(hi - lo)])
 
-        def load_adapter(g):
+        def load_h(g):
             h_sb = seg_pool.tile([P, SEG_TILES, RANK], BF16)
             nc.sync.dma_start(out=h_sb[:], in_=h_rows[g])
             h_tiles.append(h_sb)
+
+        def load_b(g):
             b_sb = seg_pool.tile([P, OUT_F], BF16)
             nc.sync.dma_start(out=b_sb[:], in_=lora_B[g])
             b_tiles.append(b_sb)
@@ -94,12 +89,15 @@ def tile_lorasequential_pa_t_kernel(tc, x, h_lora, lora_B, M_words, M_scales, ou
                     in_=M_scales[0, 4 * quadrant : 4 * quadrant + 4, :].bitcast(I32),
                 )
 
-        for g in range(N_ADAPTERS):
-            load_x(SEG_ROUNDS * g)
-            load_adapter(g)
-            load_x(SEG_ROUNDS * g + 1)
-            if g == 0:
-                load_m()
+        load_x(0, [0, 2, 4])
+        load_h(0)
+        load_b(0)
+        load_x(0, [4, 8])
+        load_m()
+        for g in range(1, N_ADAPTERS):
+            load_h(g)
+            load_x(g, [0, SEG_TILES])
+            load_b(g)
 
         hT_tiles = {}
         grouped_tiles = {}
@@ -127,7 +125,9 @@ def tile_lorasequential_pa_t_kernel(tc, x, h_lora, lora_B, M_words, M_scales, ou
                 for i in range(2):
                     for u in range(2):
                         nc.tensor.transpose(
-                            xt_ps[:, i, u, :], x_tiles[r][2 * pair + i][:, u:K_WORDS:2], ident_f32[:]
+                            xt_ps[:, i, u, :],
+                            x_tiles[r * ROUND_TILES + 2 * pair + i][:, u:K_WORDS:2],
+                            ident_f32[:],
                         )
                 nc.scalar.copy(
                     out=grouped_words[:, 2 * pair : 2 * pair + 2],
@@ -143,10 +143,18 @@ def tile_lorasequential_pa_t_kernel(tc, x, h_lora, lora_B, M_words, M_scales, ou
             )
             x_codes[r] = (codes, scales)
 
+        def store_cuts(g):
+            if g < N_ADAPTERS - 2:
+                return [0, 8]
+            if g == N_ADAPTERS - 2:
+                return [0, 4, 8]
+            return [0, 2, 4, 5, 6, 7, 8]
+
         def lora(r, i):
-            if i == 0:
-                out_sb = staged.tile([P, ROUND_TILES, OUT_F], F32)
-                out_tiles[r] = out_sb
+            g, half = divmod(r, SEG_ROUNDS)
+            if half == 0 and i == 0:
+                out_sb = staged.tile([P, SEG_TILES, OUT_F], F32)
+                out_tiles[g] = out_sb
             lora_ps = banks.tile([P, OUT_F], F32, tag="bank")
             nc.tensor.matmul(
                 out=lora_ps[:],
@@ -155,7 +163,9 @@ def tile_lorasequential_pa_t_kernel(tc, x, h_lora, lora_B, M_words, M_scales, ou
                 start=True,
                 stop=True,
             )
-            nc.scalar.mul(out=out_tiles[r][:, i, :], in_=lora_ps[:], mul=LORA_GAIN)
+            nc.scalar.mul(
+                out=out_tiles[g][:, half * ROUND_TILES + i, :], in_=lora_ps[:], mul=LORA_GAIN
+            )
 
         def base(r, i):
             codes, scales = x_codes[r]
@@ -170,15 +180,14 @@ def tile_lorasequential_pa_t_kernel(tc, x, h_lora, lora_B, M_words, M_scales, ou
                 start=True,
                 stop=True,
             )
-            out_sb = out_tiles[r]
-            nc.vector.tensor_add(out=out_sb[:, i, :], in0=base_ps[:], in1=out_sb[:, i, :])
-
-        def store(r, lo, hi):
             g, half = divmod(r, SEG_ROUNDS)
-            first = half * ROUND_TILES
-            nc.sync.dma_start(
-                out=out_rows[g][:, first + lo : first + hi, :], in_=out_tiles[r][:, lo:hi, :]
-            )
+            j = half * ROUND_TILES + i
+            out_sb = out_tiles[g]
+            nc.vector.tensor_add(out=out_sb[:, j, :], in0=base_ps[:], in1=out_sb[:, j, :])
+            cuts = store_cuts(g)
+            if j + 1 in cuts:
+                lo = cuts[cuts.index(j + 1) - 1]
+                nc.sync.dma_start(out=out_rows[g][:, lo : j + 1, :], in_=out_sb[:, lo : j + 1, :])
 
         transpose_x(0)
         transpose_h(0)
@@ -197,7 +206,3 @@ def tile_lorasequential_pa_t_kernel(tc, x, h_lora, lora_B, M_words, M_scales, ou
                 base(r, i)
                 if i == ROUND_TILES // 2 - 1 and r + 1 < ROUNDS:
                     quantise_x(r + 1)
-                if r >= ROUNDS - FINE_ROUNDS:
-                    store(r, i, i + 1)
-            if r < ROUNDS - FINE_ROUNDS:
-                store(r, 0, ROUND_TILES)

from contextlib import ExitStack

import concourse.mybir as mybir
from concourse.masks import make_identity

BF16 = mybir.dt.bfloat16
F32 = mybir.dt.float32
I32 = mybir.dt.int32
U8 = mybir.dt.uint8
U32 = mybir.dt.uint32
FP8X4 = mybir.dt.float8_e4m3fn_x4
FP4X4 = mybir.dt.float4_e2m1fn_x4

P = 128
BATCH, IN_F, OUT_F, RANK, N_ADAPTERS = 8192, 512, 512, 128, 8
LORA_GAIN = 2.0
SEG_TILES = BATCH // N_ADAPTERS // P
ROUND_TILES = 4
SEG_ROUNDS = SEG_TILES // ROUND_TILES
ROUNDS = N_ADAPTERS * SEG_ROUNDS
K_WORDS = IN_F // 2
WARM_MATMULS = 3
STAGED_SEGMENTS = 5

FLOPS = 2 * BATCH * OUT_F * (IN_F + RANK)


def tile_lorasequential_pa_t_kernel(tc, x, h_lora, lora_B, M_words, M_scales, out):
    nc = tc.nc

    x_rows = x.rearrange("(g p j) k -> g p j k", g=N_ADAPTERS, p=P)
    h_rows = h_lora.rearrange("g (p j) k -> g p j k", p=P)
    out_rows = out.rearrange("(g p j) n -> g p j n", g=N_ADAPTERS, p=P)

    with ExitStack() as ctx:
        ctx.enter_context(tc.manual_schedule())
        consts = ctx.enter_context(tc.tile_pool(name="consts", bufs=1))
        x_pool = ctx.enter_context(tc.tile_pool(name="x", bufs=N_ADAPTERS - 1))
        first_pool = ctx.enter_context(tc.tile_pool(name="first", bufs=1))
        seg_pool = ctx.enter_context(tc.tile_pool(name="seg", bufs=N_ADAPTERS))
        work = ctx.enter_context(tc.tile_pool(name="work", bufs=2))
        ht_pool = ctx.enter_context(tc.tile_pool(name="ht_sb", bufs=3))
        staged = ctx.enter_context(tc.tile_pool(name="staged", bufs=STAGED_SEGMENTS))
        banks = ctx.enter_context(tc.psum_pool(name="banks", bufs=8))

        ident_f32 = consts.tile([P, P], F32)
        make_identity(nc, ident_f32[:])
        ident_bf16 = consts.tile([P, P], BF16)
        make_identity(nc, ident_bf16[:])

        zeros = consts.tile([P, OUT_F], BF16)
        nc.vector.memset(zeros[:], 0.0)
        warm_ps = banks.tile([P, OUT_F], F32, tag="bank")
        for w in range(WARM_MATMULS):
            nc.tensor.matmul(out=warm_ps[:], lhsT=zeros[:, 0:P], rhs=zeros[:], start=True, stop=True)

        m_words = consts.tile([P, 2 * OUT_F], U8, align_bytes=64)
        m_scales = consts.tile([P, OUT_F], U8, align_bytes=64)
        nc.vector.memset(m_scales[:].bitcast(I32), 0)

        x_tiles = []
        h_tiles = []
        b_tiles = []

        def load_x(g, cuts):
            for lo, hi in zip(cuts[:-1], cuts[1:]):
                if g == 0:
                    x_sb = first_pool.tile([P, hi - lo, IN_F], BF16, name="x_first_%d" % lo)
                else:
                    x_sb = x_pool.tile([P, hi - lo, IN_F], BF16)
                nc.sync.dma_start(out=x_sb[:], in_=x_rows[g][:, lo:hi, :])
                x_tiles.extend([x_sb[:, j, :].bitcast(F32) for j in range(hi - lo)])

        def load_h(g):
            h_sb = seg_pool.tile([P, SEG_TILES, RANK], BF16)
            nc.sync.dma_start(out=h_sb[:], in_=h_rows[g])
            h_tiles.append(h_sb)

        def load_b(g):
            b_sb = seg_pool.tile([P, OUT_F], BF16)
            nc.sync.dma_start(out=b_sb[:], in_=lora_B[g])
            b_tiles.append(b_sb)

        def load_m():
            nc.sync.dma_start(out=m_words[:].bitcast(I32), in_=M_words[0].bitcast(I32))
            for quadrant in range(4):
                nc.sync.dma_start(
                    out=m_scales[32 * quadrant : 32 * quadrant + 4, :].bitcast(I32),
                    in_=M_scales[0, 4 * quadrant : 4 * quadrant + 4, :].bitcast(I32),
                )

        load_x(0, [0, 2, 4])
        load_h(0)
        load_b(0)
        load_x(0, [4, 8])
        load_m()
        for g in range(1, N_ADAPTERS):
            load_h(g)
            load_x(g, [0, SEG_TILES])
            load_b(g)

        hT_tiles = {}
        grouped_tiles = {}
        x_codes = {}
        out_tiles = {}

        def transpose_h(r):
            g, half = divmod(r, SEG_ROUNDS)
            ht_ps = banks.tile([P, ROUND_TILES, P], BF16, tag="bank")
            for i in range(ROUND_TILES):
                nc.tensor.transpose(
                    ht_ps[:, i, :], h_tiles[g][:, half * ROUND_TILES + i, :], ident_bf16[:]
                )
            hT_sb = ht_pool.tile([P, ROUND_TILES, P], BF16)
            nc.vector.tensor_copy(out=hT_sb[:], in_=ht_ps[:])
            hT_tiles[r] = hT_sb

        def transpose_x(r):
            grouped = work.tile([P, ROUND_TILES * P * 4], BF16, align_bytes=64)
            grouped_words = grouped[:].bitcast(F32).rearrange(
                "p (i r u) -> p i r u", i=ROUND_TILES, u=2
            )
            for pair in range(ROUND_TILES // 2):
                xt_ps = banks.tile([P, 2, 2, P], F32, tag="bank")
                for i in range(2):
                    for u in range(2):
                        nc.tensor.transpose(
                            xt_ps[:, i, u, :],
                            x_tiles[r * ROUND_TILES + 2 * pair + i][:, u:K_WORDS:2],
                            ident_f32[:],
                        )
                nc.scalar.copy(
                    out=grouped_words[:, 2 * pair : 2 * pair + 2],
                    in_=xt_ps[:].rearrange("p i u r -> p i r u"),
                )
            grouped_tiles[r] = grouped

        def quantise_x(r):
            codes = work.tile([P, ROUND_TILES * P], U32, align_bytes=64)
            scales = work.tile([P, ROUND_TILES * P], U8, align_bytes=64)
            nc.vector.quantize_mx(
                out=codes[:].bitcast(FP8X4), scales=scales[:], in_=grouped_tiles[r][:]
            )
            x_codes[r] = (codes, scales)

        def store_cuts(g):
            if g < N_ADAPTERS - 2:
                return [0, 8]
            if g == N_ADAPTERS - 2:
                return [0, 4, 8]
            return [0, 2, 4, 5, 6, 7, 8]

        def lora(r, i):
            g, half = divmod(r, SEG_ROUNDS)
            if half == 0 and i == 0:
                out_sb = staged.tile([P, SEG_TILES, OUT_F], F32)
                out_tiles[g] = out_sb
            lora_ps = banks.tile([P, OUT_F], F32, tag="bank")
            nc.tensor.matmul(
                out=lora_ps[:],
                lhsT=hT_tiles[r][:, i, :],
                rhs=b_tiles[r // SEG_ROUNDS][:],
                start=True,
                stop=True,
            )
            nc.scalar.mul(
                out=out_tiles[g][:, half * ROUND_TILES + i, :], in_=lora_ps[:], mul=LORA_GAIN
            )

        def base(r, i):
            codes, scales = x_codes[r]
            rows = slice(i * P, (i + 1) * P)
            base_ps = banks.tile([P, OUT_F], F32, tag="bank")
            nc.tensor.matmul_mx(
                out=base_ps[:],
                lhsT=codes[:, rows].bitcast(FP8X4),
                lhsT_scale=scales[:, rows],
                rhs=m_words[:].bitcast(FP4X4),
                rhs_scale=m_scales[:],
                start=True,
                stop=True,
            )
            g, half = divmod(r, SEG_ROUNDS)
            j = half * ROUND_TILES + i
            out_sb = out_tiles[g]
            nc.vector.tensor_add(out=out_sb[:, j, :], in0=base_ps[:], in1=out_sb[:, j, :])
            cuts = store_cuts(g)
            if j + 1 in cuts:
                lo = cuts[cuts.index(j + 1) - 1]
                nc.sync.dma_start(out=out_rows[g][:, lo : j + 1, :], in_=out_sb[:, lo : j + 1, :])

        transpose_x(0)
        transpose_h(0)
        transpose_h(1)
        quantise_x(0)
        for i in range(ROUND_TILES):
            lora(0, i)
        for r in range(ROUNDS):
            if r + 1 < ROUNDS:
                transpose_x(r + 1)
            if r + 2 < ROUNDS:
                transpose_h(r + 2)
            for i in range(ROUND_TILES):
                if r + 1 < ROUNDS:
                    lora(r + 1, i)
                base(r, i)
                if i == ROUND_TILES // 2 - 1 and r + 1 < ROUNDS:
                    quantise_x(r + 1)
